import numpy as np
import ml_dtypes


def mxq(x, axis, fmt="e4m3"):
    dtype, down = {"e4m3": (ml_dtypes.float8_e4m3fn, 7), "e5m2": (ml_dtypes.float8_e5m2, 14)}[fmt]
    v = np.moveaxis(np.asarray(x, np.float32).astype(ml_dtypes.bfloat16).astype(np.float64), axis, -1)
    blocks = v.reshape(v.shape[:-1] + (-1, 32))
    amax = np.abs(blocks).max(-1, keepdims=True)
    byte = np.maximum(np.where(amax > 0, np.frexp(amax)[1] - 1 + 127, 0) - down, 1)
    scale = np.exp2(byte - 127.0)
    codes = (blocks / scale).astype(np.float32).astype(dtype).astype(np.float64)
    return np.moveaxis((codes * scale).reshape(v.shape), -1, axis)


WIDE = False


def mx_kscale(k):
    if not WIDE:
        return np.ones(k)
    levels = np.array([10, -10, 5, -5, 0])
    a = np.random.permutation(np.resize(levels, k // 512 * 4)).reshape(k // 512, 4)
    idx = np.arange(k)
    return np.exp2(a[idx // 512, idx % 128 // 32])


BF16 = ml_dtypes.bfloat16


def bf(x):
    return np.asarray(x, np.float32).astype(BF16)


def f64(x):
    return np.asarray(x).astype(np.float64)


E2M1 = np.array([0.0, 0.5, 1.0, 1.5, 2.0, 3.0, 4.0, 6.0, -0.0, -0.5, -1.0, -1.5, -2.0, -3.0, -4.0, -6.0])


def pack_weight(w, fmt):
    k, n = w.shape
    w = f64(bf(w)).reshape(k // 32, 32, n)
    amax = np.abs(w).max(1)
    if fmt == "e4m3":
        byte = np.frexp(amax)[1] - 1 + 127 - 7
    else:
        mant, ex = np.frexp(amax / 6.0)
        byte = np.where(mant > 0.5, ex, ex - 1) + 127
    byte = np.clip(np.where(amax > 0, byte, 1), 1, 254)
    scaled = (w * np.exp2(127.0 - byte)[:, None, :]).reshape(k, n).astype(np.float32)
    by_word = np.ascontiguousarray(scaled.reshape(k // 512, 128, 4, n).transpose(0, 1, 3, 2))
    if fmt == "e4m3":
        words = by_word.astype(ml_dtypes.float8_e4m3fn).view(np.uint8)
    else:
        c = by_word.astype(ml_dtypes.float4_e2m1fn).view(np.uint8) & 0xF
        words = c[..., 0::2] | (c[..., 1::2] << 4)
    return np.ascontiguousarray(words), np.ascontiguousarray(byte.astype(np.uint8).reshape(k // 512, 16, n))


def unpack_weight(words, scales, fmt):
    g, p, n, _ = words.shape
    if fmt == "e4m3":
        vals = np.ascontiguousarray(words).view(ml_dtypes.float8_e4m3fn).astype(np.float64)
    else:
        nib = np.empty((g, p, n, 4), np.uint8)
        nib[..., 0::2] = words & 0xF
        nib[..., 1::2] = words >> 4
        vals = E2M1[nib]
    vals = vals * np.repeat(np.exp2(scales.astype(np.float64) - 127.0), 8, axis=1)[..., None]
    return vals.transpose(0, 1, 3, 2).reshape(g * 512, n)


B, D, H = 128, 2048, 1536
PASS = 512
MX_REC = H % PASS == 0


def sigmoid(v):
    return 1.0 / (1.0 + np.exp(-v))


def setup_inputs():
    s = mx_kscale(D)
    r = mx_kscale(H) if MX_REC else np.ones(H)
    gate_b = np.concatenate([np.zeros(H), np.zeros(H), np.ones(H), np.zeros(H)])
    x_t = bf(np.random.standard_normal((B, D)) * s)
    h_prev = bf(np.random.standard_normal((B, H)) * r)
    c_prev = bf(np.random.standard_normal((B, H)))
    n_prev = bf(0.5 + np.abs(np.random.standard_normal((B, H))))
    W_words, W_scales = pack_weight(np.random.standard_normal((D, 4 * H)) / np.sqrt(D) / s[:, None], "e4m3")
    R_words, R_scales = pack_weight(np.random.standard_normal((H, 4 * H)) / np.sqrt(H) / r[:, None], "e4m3")
    b = bf(gate_b + 0.2 * np.random.standard_normal(4 * H))
    return {"x_t": x_t,
            "h_prev": h_prev,
            "c_prev": c_prev,
            "n_prev": n_prev,
            "W_words": W_words,
            "W_scales": W_scales,
            "R_words": R_words,
            "R_scales": R_scales,
            "b": b}


def reference(x_t, h_prev, c_prev, n_prev, W_words, W_scales, R_words, R_scales, b):
    inp = mxq(f64(x_t), 1, "e4m3") @ unpack_weight(W_words, W_scales, "e4m3")
    if MX_REC:
        rec = mxq(f64(h_prev), 1, "e4m3") @ unpack_weight(R_words, R_scales, "e4m3")
    else:
        rec = f64(h_prev) @ unpack_weight(R_words, R_scales, "e4m3")
    pre = inp + rec + f64(b)
    z_tilde, i_tilde, f_tilde, o_tilde = np.split(pre, 4, axis=-1)
    z_t = np.tanh(z_tilde)
    i_t = np.minimum(np.exp(i_tilde), 50.0)
    f_t = sigmoid(f_tilde)
    o_t = sigmoid(o_tilde)
    c_t = f_t * f64(c_prev) + i_t * z_t
    n_t = f_t * f64(n_prev) + i_t
    h_t = o_t * (c_t / (n_t + 1e-6))
    return h_t, c_t, n_t

@@ -1,0 +1,298 @@
+from contextlib import ExitStack
+
+import concourse.mybir as mybir
+from concourse.masks import make_identity
+
+F32 = mybir.dt.float32
+BF16 = mybir.dt.bfloat16
+I32 = mybir.dt.int32
+U32 = mybir.dt.uint32
+U8 = mybir.dt.uint8
+FP8X4 = mybir.dt.float8_e4m3fn_x4
+AF = mybir.ActivationFunctionType
+ALU = mybir.AluOpType
+
+P = 128
+D_IN = 2048
+HID = 1536
+NCOL = 4 * HID
+BANK = 512
+NB = HID // BANK
+XG = D_IN // 512
+HG = HID // 512
+NPASS = XG + HG
+GATE_Z, GATE_I, GATE_F, GATE_O = 0, 1, 2, 3
+W_BUFS = 14
+EPS = 1e-6
+I_MAX = 50.0
+
+FLOPS = 2 * P * (D_IN + HID) * NCOL
+
+
+def tile_slstmcell_w_kernel(
+    tc, x_t, h_prev, c_prev, n_prev, W_words, W_scales, R_words, R_scales, b, out_0, out_1, out_2
+):
+    nc = tc.nc
+    with ExitStack() as ctx:
+        ctx.enter_context(tc.manual_schedule())
+        const = ctx.enter_context(tc.tile_pool(name="const", bufs=1))
+        wpool = ctx.enter_context(tc.tile_pool(name="wpool", bufs=W_BUFS))
+        wcpool = ctx.enter_context(tc.tile_pool(name="wcpool", bufs=NB))
+        ep = ctx.enter_context(tc.tile_pool(name="ep", bufs=1))
+        pre_pool = ctx.enter_context(tc.tile_pool(name="pre_pool", bufs=2))
+        tail = ctx.enter_context(tc.tile_pool(name="tail", bufs=NB))
+        psum = ctx.enter_context(tc.psum_pool(name="psum", bufs=8))
+
+        x_sb = const.tile([P, D_IN], BF16, name="x_sb")
+        nc.sync.dma_start(out=x_sb[:], in_=x_t)
+        h_sb = const.tile([P, HID], BF16, name="h_sb")
+        nc.sync.dma_start(out=h_sb[:], in_=h_prev)
+
+        b_rows = const.tile([P, BANK], BF16, name="b_rows")
+        nc.vector.memset(b_rows[:].bitcast(I32), 0)
+        planes_w = const.tile([P, NCOL], U8, name="planes_w", align_bytes=64)
+        nc.vector.memset(planes_w[:].bitcast(I32), 0)
+        planes_r = const.tile([P, NCOL], U8, name="planes_r", align_bytes=64)
+        nc.vector.memset(planes_r[:].bitcast(I32), 0)
+        eps = const.tile([P, 1], F32, name="eps")
+        nc.vector.memset(eps[:], EPS)
+
+        ident_f = const.tile([P, P], F32, name="ident_f")
+        make_identity(nc, ident_f[:])
+        ident_b = const.tile([P, P], BF16, name="ident_b")
+        make_identity(nc, ident_b[:])
+
+        nc.sync.dma_start(out=b_rows[0 : NCOL // BANK, :], in_=b.rearrange("(m j) -> m j", j=BANK))
+        for q in range(4):
+            nc.sync.dma_start(
+                out=planes_w[32 * q : 32 * q + 4 * XG, :].bitcast(I32),
+                in_=W_scales[:, 4 * q : 4 * q + 4, :].bitcast(I32),
+            )
+        for q in range(4):
+            nc.sync.dma_start(
+                out=planes_r[32 * q : 32 * q + 4 * HG, :].bitcast(I32),
+                in_=R_scales[:, 4 * q : 4 * q + 4, :].bitcast(I32),
+            )
+
+        c_sb = const.tile([P, HID], BF16, name="c_sb")
+        n_sb = const.tile([P, HID], BF16, name="n_sb")
+
+        def words_of(k):
+            if k < XG:
+                return W_words, k, planes_w
+            return R_words, k - XG, planes_r
+
+        loads = []
+        loaded = {}
+
+        def full_load(gate, k):
+            def go():
+                src, g = words_of(k)[0:2]
+                wt = wpool.tile([P, HID], I32, name="wt", align_bytes=64)
+                flat = src[g].rearrange("p n t -> p (n t)")
+                nc.sync.dma_start(out=wt[:], in_=flat[:, 4 * gate * HID : 4 * (gate + 1) * HID].bitcast(I32))
+                loaded[(gate, k)] = wt
+
+            return go
+
+        LAST = 2
+
+        def chunk_load(c):
+            def go():
+                wc = wcpool.tile([P, LAST, BANK], I32, name="wc", align_bytes=64)
+                flat = R_words[HG - LAST : HG].rearrange("g p n t -> p g (n t)")
+                col = GATE_O * HID + c * BANK
+                nc.sync.dma_start(out=wc[:], in_=flat[:, :, 4 * col : 4 * (col + BANK)].bitcast(I32))
+                loaded[("chunk", c)] = wc
+
+            return go
+
+        steps = []
+        for gate in (GATE_F, GATE_I, GATE_Z):
+            for k in range(NPASS):
+                loads.append(full_load(gate, k))
+                steps.append((gate, k))
+        for k in range(NPASS - LAST):
+            loads.append(full_load(GATE_O, k))
+            steps.append((GATE_O, k))
+        for c in range(NB):
+            loads.append(chunk_load(c))
+            steps.append(("chunk", c))
+
+        n_issued = 0
+        for i in range(W_BUFS):
+            loads[i]()
+            n_issued += 1
+            if i == 3:
+                nc.sync.dma_start(out=n_sb[:], in_=n_prev)
+                nc.sync.dma_start(out=c_sb[:], in_=c_prev)
+
+        grouped = const.tile([P, NPASS * 512], BF16, name="grouped", align_bytes=64)
+        grouped_w = grouped[:].bitcast(F32)
+        codes = const.tile([P, NPASS * P], U32, name="codes", align_bytes=64)
+        xplane = const.tile([P, NPASS * P], U8, name="xplane", align_bytes=64)
+
+        def transposes(src_sb, g_list):
+            bank = psum.tile([P, 4, P], F32, name="tp", tag="bank")
+            words = src_sb[:].bitcast(F32)
+            for j, g in enumerate(g_list):
+                for u in range(2):
+                    nc.tensor.transpose(bank[:, 2 * j + u, :], words[:, 256 * g + u : 256 * (g + 1) : 2], ident_f[:])
+            return bank
+
+        def copy_out(engine_copy, bank, first_pass, n):
+            dst = grouped_w[:, 256 * first_pass : 256 * (first_pass + n)].rearrange(
+                "p (g r u) -> p g r u", g=n, r=P, u=2
+            )
+            src = bank[:, 0 : 2 * n, :].rearrange("p (g u) r -> p g r u", g=n, u=2)
+            engine_copy(out=dst, in_=src)
+
+        xb0 = transposes(x_sb, [0, 1])
+        xb1 = transposes(x_sb, [2, 3])
+        hb0 = transposes(h_sb, [0, 1])
+        hb1 = transposes(h_sb, [2])
+        copy_out(nc.vector.tensor_copy, xb0, 0, 2)
+        copy_out(nc.vector.tensor_copy, xb1, 2, 2)
+        copy_out(nc.scalar.copy, hb0, 4, 2)
+        copy_out(nc.scalar.copy, hb1, 6, 1)
+
+        def quantise(first_pass, n):
+            nc.vector.quantize_mx(
+                out=codes[:, P * first_pass : P * (first_pass + n)].bitcast(FP8X4),
+                scales=xplane[:, P * first_pass : P * (first_pass + n)],
+                in_=grouped[:, 512 * first_pass : 512 * (first_pass + n)],
+            )
+
+        quantise(0, 4)
+
+        bias = const.tile([P, NCOL], BF16, name="bias")
+        for m in range(NCOL // BANK):
+            bp = psum.tile([P, BANK], F32, name="bp", tag="bank")
+            nc.tensor.matmul(
+                out=bp[:], lhsT=ident_b[:, m : m + 1].to_broadcast([P, P]), rhs=b_rows[:], start=True, stop=True
+            )
+            if m % 2 == 0:
+                nc.vector.tensor_copy(out=bias[:, BANK * m : BANK * (m + 1)], in_=bp[:])
+            else:
+                nc.scalar.copy(out=bias[:, BANK * m : BANK * (m + 1)], in_=bp[:])
+            if m == 0:
+                quantise(4, 2)
+            if m == 2:
+                quantise(6, 1)
+
+        acc = {}
+        f_s = ep.tile([P, HID], F32, name="f_s")
+        e_s = ep.tile([P, HID], F32, name="e_s")
+        z_s = ep.tile([P, HID], F32, name="z_s")
+        n_new = ep.tile([P, HID], F32, name="n_new")
+        c_new = ep.tile([P, HID], F32, name="c_new")
+        rs = ep.tile([P, HID], F32, name="rs")
+        quot = ep.tile([P, HID], F32, name="quot")
+
+        def mx_pass(out_bank, k, rhs, col, start, stop):
+            g, planes = words_of(k)[1:3]
+            nc.tensor.matmul_mx(
+                out=out_bank[:],
+                lhsT=codes[:, P * k : P * (k + 1)].bitcast(FP8X4),
+                lhsT_scale=xplane[:, P * k : P * (k + 1)],
+                rhs=rhs.bitcast(FP8X4),
+                rhs_scale=planes[4 * g : P, col : col + BANK],
+                start=start,
+                stop=stop,
+            )
+
+        def cols(c):
+            return slice(BANK * c, BANK * (c + 1))
+
+        def pre_act(gate, func, dst):
+            pre = pre_pool.tile([P, HID], F32, name="pre")
+            for c in range(NB):
+                nc.vector.tensor_tensor(
+                    out=pre[:, cols(c)],
+                    in0=acc[(gate, c)][:],
+                    in1=bias[:, gate * HID + BANK * c : gate * HID + BANK * (c + 1)],
+                    op=ALU.add,
+                )
+                nc.scalar.activation(out=dst[:, cols(c)], in_=pre[:, cols(c)], func=func)
+
+        def after_f():
+            pre_act(GATE_F, AF.Sigmoid, f_s)
+            nc.vector.tensor_tensor(out=n_new[:], in0=f_s[:], in1=n_sb[:], op=ALU.mult)
+            nc.vector.tensor_tensor(out=c_new[:], in0=f_s[:], in1=c_sb[:], op=ALU.mult)
+
+        def after_i():
+            pre_act(GATE_I, AF.Exp, e_s)
+            for c in range(NB):
+                nc.vector.scalar_tensor_tensor(
+                    out=n_new[:, cols(c)], in0=e_s[:, cols(c)], scalar=I_MAX, in1=n_new[:, cols(c)],
+                    op0=ALU.min, op1=ALU.add,
+                )
+                nc.scalar.activation(
+                    out=rs[:, cols(c)], in_=n_new[:, cols(c)], func=AF.Abs_reciprocal_sqrt, bias=eps[:]
+                )
+            nc.gpsimd.dma_start(out=out_2, in_=n_new[:])
+            nc.scalar.activation(out=rs[:], in_=rs[:], func=AF.Square)
+            nc.scalar.activation(out=rs[:], in_=rs[:], func=AF.Square)
+            nc.vector.scalar_tensor_tensor(
+                out=quot[:], in0=n_new[:], scalar=EPS, in1=rs[:], op0=ALU.add, op1=ALU.mult
+            )
+
+        def after_z():
+            pre_act(GATE_Z, AF.Tanh, z_s)
+            for c in range(NB):
+                nc.vector.scalar_tensor_tensor(
+                    out=z_s[:, cols(c)], in0=e_s[:, cols(c)], scalar=I_MAX, in1=z_s[:, cols(c)],
+                    op0=ALU.min, op1=ALU.mult,
+                )
+                nc.vector.tensor_tensor(
+                    out=c_new[:, cols(c)], in0=c_new[:, cols(c)], in1=z_s[:, cols(c)], op=ALU.add
+                )
+                nc.vector.tensor_tensor(
+                    out=quot[:, cols(c)], in0=quot[:, cols(c)], in1=c_new[:, cols(c)], op=ALU.mult
+                )
+            nc.gpsimd.dma_start(out=out_1, in_=c_new[:])
+
+        o_s = {}
+
+        def o_front(c):
+            pre = tail.tile([P, BANK], F32, name="pre_o")
+            col = GATE_O * HID + BANK * c
+            nc.vector.tensor_tensor(
+                out=pre[:], in0=acc[(GATE_O, c)][:], in1=bias[:, col : col + BANK], op=ALU.add
+            )
+            o_s[c] = tail.tile([P, BANK], F32, name="o_s")
+            nc.scalar.activation(out=o_s[c][:], in_=pre[:], func=AF.Sigmoid)
+
+        def o_back(c):
+            h_new = tail.tile([P, BANK], F32, name="h_new")
+            nc.vector.tensor_tensor(out=h_new[:], in0=o_s[c][:], in1=quot[:, cols(c)], op=ALU.mult)
+            nc.sync.dma_start(out=out_0[:, cols(c)], in_=h_new[:])
+
+        after = {GATE_F: after_f, GATE_I: after_i, GATE_Z: after_z}
+
+        for i, step in enumerate(steps):
+            if step[0] == "chunk":
+                c = step[1]
+                wc = loaded[step]
+                for j in range(LAST):
+                    k = NPASS - LAST + j
+                    mx_pass(acc[(GATE_O, c)], k, wc[:, j, :], GATE_O * HID + BANK * c, False, j == LAST - 1)
+                o_front(c)
+                if c > 0:
+                    o_back(c - 1)
+            else:
+                gate, k = step
+                wt = loaded[step]
+                for c in range(NB):
+                    if k == 0:
+                        acc[(gate, c)] = psum.tile([P, BANK], F32, name="acc", tag="bank")
+                    mx_pass(
+                        acc[(gate, c)], k, wt[:, cols(c)], gate * HID + BANK * c, k == 0,
+                        k == NPASS - 1,
+                    )
+                if k == NPASS - 1:
+                    after[gate]()
+            if n_issued < len(loads):
+                loads[n_issued]()
+                n_issued += 1
+        o_back(NB - 1)

@@ -230,7 +230,6 @@ def tile_slstmcell_w_kernel(
                 nc.scalar.activation(
                     out=rs[:, cols(c)], in_=n_new[:, cols(c)], func=AF.Abs_reciprocal_sqrt, bias=eps[:]
                 )
-            nc.gpsimd.dma_start(out=out_2, in_=n_new[:])
             nc.scalar.activation(out=rs[:], in_=rs[:], func=AF.Square)
             nc.scalar.activation(out=rs[:], in_=rs[:], func=AF.Square)
             nc.vector.scalar_tensor_tensor(
@@ -250,7 +249,8 @@ def tile_slstmcell_w_kernel(
                 nc.vector.tensor_tensor(
                     out=quot[:, cols(c)], in0=quot[:, cols(c)], in1=c_new[:, cols(c)], op=ALU.mult
                 )
-            nc.gpsimd.dma_start(out=out_1, in_=c_new[:])
+            nc.sync.dma_start(out=out_2, in_=n_new[:])
+            nc.sync.dma_start(out=out_1, in_=c_new[:])
 
         o_s = {}
 

@@ -62,16 +62,16 @@ def tile_slstmcell_w_kernel(
         ident_b = const.tile([P, P], BF16, name="ident_b")
         make_identity(nc, ident_b[:])
 
-        nc.sync.dma_start(out=b_rows[0 : NCOL // BANK, :], in_=b.rearrange("(m j) -> m j", j=BANK))
-        for q in range(4):
-            nc.sync.dma_start(
-                out=planes_w[32 * q : 32 * q + 4 * XG, :].bitcast(I32),
-                in_=W_scales[:, 4 * q : 4 * q + 4, :].bitcast(I32),
+        nc.scalar.dma_start(out=b_rows[0 : NCOL // BANK, :], in_=b.rearrange("(m j) -> m j", j=BANK))
+        for q in (0, 2, 1, 3):
+            nc.gpsimd.dma_start(
+                out=planes_w[32 * q : 32 * q + 4 * XG, :].bitcast(F32),
+                in_=W_scales[:, 4 * q : 4 * q + 4, :].bitcast(F32),
             )
-        for q in range(4):
-            nc.sync.dma_start(
-                out=planes_r[32 * q : 32 * q + 4 * HG, :].bitcast(I32),
-                in_=R_scales[:, 4 * q : 4 * q + 4, :].bitcast(I32),
+        for q in (0, 2, 1, 3):
+            nc.gpsimd.dma_start(
+                out=planes_r[32 * q : 32 * q + 4 * HG, :].bitcast(F32),
+                in_=R_scales[:, 4 * q : 4 * q + 4, :].bitcast(F32),
             )
 
         c_sb = const.tile([P, HID], BF16, name="c_sb")

@@ -62,17 +62,16 @@ def tile_slstmcell_w_kernel(
         ident_b = const.tile([P, P], BF16, name="ident_b")
         make_identity(nc, ident_b[:])
 
-        nc.scalar.dma_start(out=b_rows[0 : NCOL // BANK, :], in_=b.rearrange("(m j) -> m j", j=BANK))
-        for q in (0, 2, 1, 3):
-            nc.gpsimd.dma_start(
-                out=planes_w[32 * q : 32 * q + 4 * XG, :].bitcast(F32),
-                in_=W_scales[:, 4 * q : 4 * q + 4, :].bitcast(F32),
-            )
-        for q in (0, 2, 1, 3):
-            nc.gpsimd.dma_start(
-                out=planes_r[32 * q : 32 * q + 4 * HG, :].bitcast(F32),
-                in_=R_scales[:, 4 * q : 4 * q + 4, :].bitcast(F32),
-            )
+        nc.sync.dma_start(out=b_rows[0 : NCOL // BANK, :], in_=b.rearrange("(m j) -> m j", j=BANK))
+        SCALE_CUT = 2
+        piece = NCOL // SCALE_CUT
+        for planes, scales, groups in ((planes_w, W_scales, XG), (planes_r, R_scales, HG)):
+            for q in range(4):
+                for s in range(SCALE_CUT):
+                    nc.sync.dma_start(
+                        out=planes[32 * q : 32 * q + 4 * groups, piece * s : piece * (s + 1)].bitcast(I32),
+                        in_=scales[:, 4 * q : 4 * q + 4, piece * s : piece * (s + 1)].bitcast(I32),
+                    )
 
         c_sb = const.tile([P, HID], BF16, name="c_sb")
         n_sb = const.tile([P, HID], BF16, name="n_sb")

@@ -48,12 +48,12 @@ def tile_slstmcell_w_kernel(
         h_sb = const.tile([P, HID], BF16, name="h_sb")
         nc.sync.dma_start(out=h_sb[:], in_=h_prev)
 
-        b_rows = const.tile([P, BANK], BF16, name="b_rows")
-        nc.vector.memset(b_rows[:].bitcast(I32), 0)
         planes_w = const.tile([P, NCOL], U8, name="planes_w", align_bytes=64)
         nc.vector.memset(planes_w[:].bitcast(I32), 0)
         planes_r = const.tile([P, NCOL], U8, name="planes_r", align_bytes=64)
         nc.vector.memset(planes_r[:].bitcast(I32), 0)
+        b_rows = const.tile([P, BANK], BF16, name="b_rows")
+        nc.vector.memset(b_rows[:].bitcast(I32), 0)
         eps = const.tile([P, 1], F32, name="eps")
         nc.vector.memset(eps[:], EPS)
 
@@ -62,16 +62,13 @@ def tile_slstmcell_w_kernel(
         ident_b = const.tile([P, P], BF16, name="ident_b")
         make_identity(nc, ident_b[:])
 
-        nc.sync.dma_start(out=b_rows[0 : NCOL // BANK, :], in_=b.rearrange("(m j) -> m j", j=BANK))
-        SCALE_CUT = 2
-        piece = NCOL // SCALE_CUT
-        for planes, scales, groups in ((planes_w, W_scales, XG), (planes_r, R_scales, HG)):
-            for q in range(4):
-                for s in range(SCALE_CUT):
-                    nc.sync.dma_start(
-                        out=planes[32 * q : 32 * q + 4 * groups, piece * s : piece * (s + 1)].bitcast(I32),
-                        in_=scales[:, 4 * q : 4 * q + 4, piece * s : piece * (s + 1)].bitcast(I32),
-                    )
+        nc.scalar.dma_start(out=b_rows[0 : NCOL // BANK, :], in_=b.rearrange("(m j) -> m j", j=BANK))
+
+        def scale_load(planes, scales, groups, q):
+            nc.sync.dma_start(
+                out=planes[32 * q : 32 * q + 4 * groups, :].bitcast(I32),
+                in_=scales[:, 4 * q : 4 * q + 4, :].bitcast(I32),
+            )
 
         c_sb = const.tile([P, HID], BF16, name="c_sb")
         n_sb = const.tile([P, HID], BF16, name="n_sb")
@@ -122,7 +119,11 @@ def tile_slstmcell_w_kernel(
         for i in range(W_BUFS):
             loads[i]()
             n_issued += 1
-            if i == 3:
+            if i < 4:
+                scale_load(planes_w, W_scales, XG, i)
+            elif i < 8:
+                scale_load(planes_r, R_scales, HG, i - 4)
+            elif i == 8:
                 nc.sync.dma_start(out=n_sb[:], in_=n_prev)
                 nc.sync.dma_start(out=c_sb[:], in_=c_prev)
 

@@ -54,6 +54,11 @@ def tile_slstmcell_w_kernel(
         nc.vector.memset(planes_r[:].bitcast(I32), 0)
         b_rows = const.tile([P, BANK], BF16, name="b_rows")
         nc.vector.memset(b_rows[:].bitcast(I32), 0)
+        for q in (0, 2, 1, 3):
+            nc.gpsimd.dma_start(
+                out=planes_w[32 * q : 32 * q + 4 * XG, :].bitcast(F32),
+                in_=W_scales[:, 4 * q : 4 * q + 4, :].bitcast(F32),
+            )
         eps = const.tile([P, 1], F32, name="eps")
         nc.vector.memset(eps[:], EPS)
 
@@ -61,14 +66,13 @@ def tile_slstmcell_w_kernel(
         make_identity(nc, ident_f[:])
         ident_b = const.tile([P, P], BF16, name="ident_b")
         make_identity(nc, ident_b[:])
+        for q in (0, 2, 1, 3):
+            nc.gpsimd.dma_start(
+                out=planes_r[32 * q : 32 * q + 4 * HG, :].bitcast(F32),
+                in_=R_scales[:, 4 * q : 4 * q + 4, :].bitcast(F32),
+            )
 
         nc.scalar.dma_start(out=b_rows[0 : NCOL // BANK, :], in_=b.rearrange("(m j) -> m j", j=BANK))
-
-        def scale_load(planes, scales, groups, q):
-            nc.sync.dma_start(
-                out=planes[32 * q : 32 * q + 4 * groups, :].bitcast(I32),
-                in_=scales[:, 4 * q : 4 * q + 4, :].bitcast(I32),
-            )
 
         c_sb = const.tile([P, HID], BF16, name="c_sb")
         n_sb = const.tile([P, HID], BF16, name="n_sb")
@@ -119,11 +123,7 @@ def tile_slstmcell_w_kernel(
         for i in range(W_BUFS):
             loads[i]()
             n_issued += 1
-            if i < 4:
-                scale_load(planes_w, W_scales, XG, i)
-            elif i < 8:
-                scale_load(planes_r, R_scales, HG, i - 4)
-            elif i == 8:
+            if i == 3:
                 nc.sync.dma_start(out=n_sb[:], in_=n_prev)
                 nc.sync.dma_start(out=c_sb[:], in_=c_prev)
 

@@ -246,27 +246,39 @@ def tile_slstmcell_w_kernel(
                 nc.vector.tensor_tensor(
                     out=c_new[:, cols(c)], in0=c_new[:, cols(c)], in1=z_s[:, cols(c)], op=ALU.add
                 )
-                nc.vector.tensor_tensor(
-                    out=quot[:, cols(c)], in0=quot[:, cols(c)], in1=c_new[:, cols(c)], op=ALU.mult
+                nc.vector.scalar_tensor_tensor(
+                    out=quot[:, cols(c)], in0=quot[:, cols(c)], scalar=0.5, in1=c_new[:, cols(c)],
+                    op0=ALU.mult, op1=ALU.mult,
                 )
             nc.sync.dma_start(out=out_2, in_=n_new[:])
             nc.sync.dma_start(out=out_1, in_=c_new[:])
 
         o_s = {}
+        h_new = {}
+
+        def pieces(c):
+            if c == NB - 1:
+                return (slice(0, BANK // 2), slice(BANK // 2, BANK))
+            return (slice(0, BANK),)
 
         def o_front(c):
             pre = tail.tile([P, BANK], F32, name="pre_o")
             col = GATE_O * HID + BANK * c
-            nc.vector.tensor_tensor(
-                out=pre[:], in0=acc[(GATE_O, c)][:], in1=bias[:, col : col + BANK], op=ALU.add
-            )
             o_s[c] = tail.tile([P, BANK], F32, name="o_s")
-            nc.scalar.activation(out=o_s[c][:], in_=pre[:], func=AF.Sigmoid)
+            for s in pieces(c):
+                nc.vector.tensor_tensor(
+                    out=pre[:, s], in0=acc[(GATE_O, c)][:, s], in1=bias[:, col + s.start : col + s.stop], op=ALU.add
+                )
+                nc.scalar.activation(out=o_s[c][:, s], in_=pre[:, s], func=AF.Tanh, scale=0.5)
 
         def o_back(c):
-            h_new = tail.tile([P, BANK], F32, name="h_new")
-            nc.vector.tensor_tensor(out=h_new[:], in0=o_s[c][:], in1=quot[:, cols(c)], op=ALU.mult)
-            nc.sync.dma_start(out=out_0[:, cols(c)], in_=h_new[:])
+            h_new[c] = tail.tile([P, BANK], F32, name="h_new")
+            for s in pieces(c):
+                nc.vector.scalar_tensor_tensor(
+                    out=h_new[c][:, s], in0=o_s[c][:, s], scalar=1.0,
+                    in1=quot[:, BANK * c + s.start : BANK * c + s.stop], op0=ALU.add, op1=ALU.mult,
+                )
+            nc.sync.dma_start(out=out_0[:, cols(c)], in_=h_new[c][:])
 
         after = {GATE_F: after_f, GATE_I: after_i, GATE_Z: after_z}
 

@@ -1,7 +1,6 @@
 from contextlib import ExitStack
 
 import concourse.mybir as mybir
-from concourse.masks import make_identity
 
 F32 = mybir.dt.float32
 BF16 = mybir.dt.bfloat16
@@ -22,7 +21,9 @@ XG = D_IN // 512
 HG = HID // 512
 NPASS = XG + HG
 GATE_Z, GATE_I, GATE_F, GATE_O = 0, 1, 2, 3
-W_BUFS = 14
+APART = 2
+W_BUFS = 9
+AHEAD = 9
 EPS = 1e-6
 I_MAX = 50.0
 
@@ -37,9 +38,10 @@ def tile_slstmcell_w_kernel(
         ctx.enter_context(tc.manual_schedule())
         const = ctx.enter_context(tc.tile_pool(name="const", bufs=1))
         wpool = ctx.enter_context(tc.tile_pool(name="wpool", bufs=W_BUFS))
+        pairpool = ctx.enter_context(tc.tile_pool(name="pairpool", bufs=NPASS - APART))
         wcpool = ctx.enter_context(tc.tile_pool(name="wcpool", bufs=NB))
         ep = ctx.enter_context(tc.tile_pool(name="ep", bufs=1))
-        pre_pool = ctx.enter_context(tc.tile_pool(name="pre_pool", bufs=2))
+        pre_pool = ctx.enter_context(tc.tile_pool(name="pre_pool", bufs=NB))
         tail = ctx.enter_context(tc.tile_pool(name="tail", bufs=NB))
         psum = ctx.enter_context(tc.psum_pool(name="psum", bufs=8))
 
@@ -63,9 +65,13 @@ def tile_slstmcell_w_kernel(
         nc.vector.memset(eps[:], EPS)
 
         ident_f = const.tile([P, P], F32, name="ident_f")
-        make_identity(nc, ident_f[:])
+        nc.vector.memset(ident_f[:], 0.0)
+        nc.gpsimd.affine_select(
+            out=ident_f[:], in_=ident_f[:], compare_op=ALU.not_equal, fill=1.0, base=0,
+            pattern=[[-1, P]], channel_multiplier=1,
+        )
         ident_b = const.tile([P, P], BF16, name="ident_b")
-        make_identity(nc, ident_b[:])
+        nc.vector.tensor_copy(out=ident_b[:], in_=ident_f[:])
         for q in (0, 2, 1, 3):
             nc.gpsimd.dma_start(
                 out=planes_r[32 * q : 32 * q + 4 * HG, :].bitcast(F32),
@@ -97,6 +103,16 @@ def tile_slstmcell_w_kernel(
 
         LAST = 2
 
+        def pair_load(k):
+            def go():
+                src, g = words_of(k)[0:2]
+                wt = pairpool.tile([P, 2 * HID], I32, name="wp", align_bytes=64)
+                flat = src[g].rearrange("p n t -> p (n t)")
+                nc.sync.dma_start(out=wt[:], in_=flat[:, 4 * GATE_I * HID : 4 * (GATE_F + 1) * HID].bitcast(I32))
+                loaded[("pair", k)] = wt
+
+            return go
+
         def chunk_load(c):
             def go():
                 wc = wcpool.tile([P, LAST, BANK], I32, name="wc", align_bytes=64)
@@ -108,10 +124,16 @@ def tile_slstmcell_w_kernel(
             return go
 
         steps = []
-        for gate in (GATE_F, GATE_I, GATE_Z):
-            for k in range(NPASS):
+        for k in range(APART):
+            for gate in (GATE_I, GATE_F):
                 loads.append(full_load(gate, k))
                 steps.append((gate, k))
+        for k in range(APART, NPASS):
+            loads.append(pair_load(k))
+            steps.append(("pair", k))
+        for k in range(NPASS):
+            loads.append(full_load(GATE_Z, k))
+            steps.append((GATE_Z, k))
         for k in range(NPASS - LAST):
             loads.append(full_load(GATE_O, k))
             steps.append((GATE_O, k))
@@ -120,7 +142,7 @@ def tile_slstmcell_w_kernel(
             steps.append(("chunk", c))
 
         n_issued = 0
-        for i in range(W_BUFS):
+        for i in range(NPASS - APART + W_BUFS):
             loads[i]()
             n_issued += 1
             if i == 3:
@@ -180,6 +202,9 @@ def tile_slstmcell_w_kernel(
             if m == 2:
                 quantise(6, 1)
 
+        nc.scalar.mul(n_sb[:], n_sb[:], 0.5)
+        nc.scalar.mul(c_sb[:], c_sb[:], 0.5)
+
         acc = {}
         f_s = ep.tile([P, HID], F32, name="f_s")
         e_s = ep.tile([P, HID], F32, name="e_s")
@@ -187,7 +212,6 @@ def tile_slstmcell_w_kernel(
         n_new = ep.tile([P, HID], F32, name="n_new")
         c_new = ep.tile([P, HID], F32, name="c_new")
         rs = ep.tile([P, HID], F32, name="rs")
-        quot = ep.tile([P, HID], F32, name="quot")
 
         def mx_pass(out_bank, k, rhs, col, start, stop):
             g, planes = words_of(k)[1:3]
@@ -204,25 +228,29 @@ def tile_slstmcell_w_kernel(
         def cols(c):
             return slice(BANK * c, BANK * (c + 1))
 
-        def pre_act(gate, func, dst):
-            pre = pre_pool.tile([P, HID], F32, name="pre")
+        def pre_act(gate, func, scale, dst):
             for c in range(NB):
+                pre = pre_pool.tile([P, BANK], F32, name="pre")
                 nc.vector.tensor_tensor(
-                    out=pre[:, cols(c)],
+                    out=pre[:],
                     in0=acc[(gate, c)][:],
                     in1=bias[:, gate * HID + BANK * c : gate * HID + BANK * (c + 1)],
                     op=ALU.add,
                 )
-                nc.scalar.activation(out=dst[:, cols(c)], in_=pre[:, cols(c)], func=func)
+                nc.scalar.activation(out=dst[:, cols(c)], in_=pre[:], func=func, scale=scale)
 
-        def after_f():
-            pre_act(GATE_F, AF.Sigmoid, f_s)
-            nc.vector.tensor_tensor(out=n_new[:], in0=f_s[:], in1=n_sb[:], op=ALU.mult)
-            nc.vector.tensor_tensor(out=c_new[:], in0=f_s[:], in1=c_sb[:], op=ALU.mult)
-
-        def after_i():
-            pre_act(GATE_I, AF.Exp, e_s)
+        def after_i_and_f():
+            pre_act(GATE_I, AF.Exp, 1.0, e_s)
+            pre_act(GATE_F, AF.Tanh, 0.5, f_s)
             for c in range(NB):
+                nc.vector.scalar_tensor_tensor(
+                    out=n_new[:, cols(c)], in0=f_s[:, cols(c)], scalar=1.0, in1=n_sb[:, cols(c)],
+                    op0=ALU.add, op1=ALU.mult,
+                )
+                nc.vector.scalar_tensor_tensor(
+                    out=c_new[:, cols(c)], in0=f_s[:, cols(c)], scalar=1.0, in1=c_sb[:, cols(c)],
+                    op0=ALU.add, op1=ALU.mult,
+                )
                 nc.vector.scalar_tensor_tensor(
                     out=n_new[:, cols(c)], in0=e_s[:, cols(c)], scalar=I_MAX, in1=n_new[:, cols(c)],
                     op0=ALU.min, op1=ALU.add,
@@ -230,14 +258,16 @@ def tile_slstmcell_w_kernel(
                 nc.scalar.activation(
                     out=rs[:, cols(c)], in_=n_new[:, cols(c)], func=AF.Abs_reciprocal_sqrt, bias=eps[:]
                 )
-            nc.scalar.activation(out=rs[:], in_=rs[:], func=AF.Square)
-            nc.scalar.activation(out=rs[:], in_=rs[:], func=AF.Square)
-            nc.vector.scalar_tensor_tensor(
-                out=quot[:], in0=n_new[:], scalar=EPS, in1=rs[:], op0=ALU.add, op1=ALU.mult
-            )
+                nc.scalar.activation(out=rs[:, cols(c)], in_=rs[:, cols(c)], func=AF.Square)
+                nc.scalar.activation(out=rs[:, cols(c)], in_=rs[:, cols(c)], func=AF.Square)
+            for c in range(NB):
+                nc.vector.scalar_tensor_tensor(
+                    out=rs[:, cols(c)], in0=n_new[:, cols(c)], scalar=EPS, in1=rs[:, cols(c)],
+                    op0=ALU.add, op1=ALU.mult,
+                )
 
         def after_z():
-            pre_act(GATE_Z, AF.Tanh, z_s)
+            pre_act(GATE_Z, AF.Tanh, 1.0, z_s)
             for c in range(NB):
                 nc.vector.scalar_tensor_tensor(
                     out=z_s[:, cols(c)], in0=e_s[:, cols(c)], scalar=I_MAX, in1=z_s[:, cols(c)],
@@ -247,7 +277,7 @@ def tile_slstmcell_w_kernel(
                     out=c_new[:, cols(c)], in0=c_new[:, cols(c)], in1=z_s[:, cols(c)], op=ALU.add
                 )
                 nc.vector.scalar_tensor_tensor(
-                    out=quot[:, cols(c)], in0=quot[:, cols(c)], scalar=0.5, in1=c_new[:, cols(c)],
+                    out=rs[:, cols(c)], in0=rs[:, cols(c)], scalar=0.5, in1=c_new[:, cols(c)],
                     op0=ALU.mult, op1=ALU.mult,
                 )
             nc.sync.dma_start(out=out_2, in_=n_new[:])
@@ -276,11 +306,11 @@ def tile_slstmcell_w_kernel(
             for s in pieces(c):
                 nc.vector.scalar_tensor_tensor(
                     out=h_new[c][:, s], in0=o_s[c][:, s], scalar=1.0,
-                    in1=quot[:, BANK * c + s.start : BANK * c + s.stop], op0=ALU.add, op1=ALU.mult,
+                    in1=rs[:, BANK * c + s.start : BANK * c + s.stop], op0=ALU.add, op1=ALU.mult,
                 )
             nc.sync.dma_start(out=out_0[:, cols(c)], in_=h_new[c][:])
 
-        after = {GATE_F: after_f, GATE_I: after_i, GATE_Z: after_z}
+        after = {"pair": after_i_and_f, GATE_Z: after_z}
 
         for i, step in enumerate(steps):
             if step[0] == "chunk":
@@ -293,18 +323,20 @@ def tile_slstmcell_w_kernel(
                 if c > 0:
                     o_back(c - 1)
             else:
-                gate, k = step
+                k = step[1]
                 wt = loaded[step]
-                for c in range(NB):
-                    if k == 0:
-                        acc[(gate, c)] = psum.tile([P, BANK], F32, name="acc", tag="bank")
-                    mx_pass(
-                        acc[(gate, c)], k, wt[:, cols(c)], gate * HID + BANK * c, k == 0,
-                        k == NPASS - 1,
-                    )
+                gates = (GATE_I, GATE_F) if step[0] == "pair" else (step[0],)
+                for j, gate in enumerate(gates):
+                    for c in range(NB):
+                        if k == 0:
+                            acc[(gate, c)] = psum.tile([P, BANK], F32, name="acc", tag="bank")
+                        mx_pass(
+                            acc[(gate, c)], k, wt[:, j * HID + BANK * c : j * HID + BANK * (c + 1)],
+                            gate * HID + BANK * c, k == 0, k == NPASS - 1,
+                        )
                 if k == NPASS - 1:
-                    after[gate]()
-            if n_issued < len(loads):
+                    after[step[0]]()
+            if n_issued <= i + AHEAD and n_issued < len(loads):
                 loads[n_issued]()
                 n_issued += 1
         o_back(NB - 1)

@@ -42,7 +42,6 @@ def tile_slstmcell_w_kernel(
         wcpool = ctx.enter_context(tc.tile_pool(name="wcpool", bufs=NB))
         ep = ctx.enter_context(tc.tile_pool(name="ep", bufs=1))
         pre_pool = ctx.enter_context(tc.tile_pool(name="pre_pool", bufs=NB))
-        tail = ctx.enter_context(tc.tile_pool(name="tail", bufs=NB))
         psum = ctx.enter_context(tc.psum_pool(name="psum", bufs=8))
 
         x_sb = const.tile([P, D_IN], BF16, name="x_sb")
@@ -83,6 +82,9 @@ def tile_slstmcell_w_kernel(
         c_sb = const.tile([P, HID], BF16, name="c_sb")
         n_sb = const.tile([P, HID], BF16, name="n_sb")
 
+        def cols(c):
+            return slice(BANK * c, BANK * (c + 1))
+
         def words_of(k):
             if k < XG:
                 return W_words, k, planes_w
@@ -101,8 +103,6 @@ def tile_slstmcell_w_kernel(
 
             return go
 
-        LAST = 2
-
         def pair_load(k):
             def go():
                 src, g = words_of(k)[0:2]
@@ -113,13 +113,25 @@ def tile_slstmcell_w_kernel(
 
             return go
 
-        def chunk_load(c):
+        FULL_O = NPASS - HG
+
+        def left_load(k):
             def go():
-                wc = wcpool.tile([P, LAST, BANK], I32, name="wc", align_bytes=64)
-                flat = R_words[HG - LAST : HG].rearrange("g p n t -> p g (n t)")
-                col = GATE_O * HID + c * BANK
-                nc.sync.dma_start(out=wc[:], in_=flat[:, :, 4 * col : 4 * (col + BANK)].bitcast(I32))
-                loaded[("chunk", c)] = wc
+                wl = wcpool.tile([P, 2 * BANK], I32, name="wl", align_bytes=64)
+                flat = R_words[k - XG].rearrange("p n t -> p (n t)")
+                col = GATE_O * HID
+                nc.sync.dma_start(out=wl[:], in_=flat[:, 4 * col : 4 * (col + 2 * BANK)].bitcast(I32))
+                loaded[("left", k)] = [wl[:, cols(0)], wl[:, cols(1)]]
+
+            return go
+
+        def right_load(k):
+            def go():
+                wr = wcpool.tile([P, BANK], I32, name="wr", align_bytes=64)
+                flat = R_words[k - XG].rearrange("p n t -> p (n t)")
+                col = GATE_O * HID + 2 * BANK
+                nc.sync.dma_start(out=wr[:], in_=flat[:, 4 * col : 4 * (col + BANK)].bitcast(I32))
+                loaded[("right", k)] = [wr[:]]
 
             return go
 
@@ -134,12 +146,13 @@ def tile_slstmcell_w_kernel(
         for k in range(NPASS):
             loads.append(full_load(GATE_Z, k))
             steps.append((GATE_Z, k))
-        for k in range(NPASS - LAST):
+        for k in range(FULL_O):
             loads.append(full_load(GATE_O, k))
             steps.append((GATE_O, k))
-        for c in range(NB):
-            loads.append(chunk_load(c))
-            steps.append(("chunk", c))
+        for part, load in (("left", left_load), ("right", right_load)):
+            for k in range(FULL_O, NPASS):
+                loads.append(load(k))
+                steps.append((part, k))
 
         n_issued = 0
         for i in range(NPASS - APART + W_BUFS):
@@ -225,32 +238,26 @@ def tile_slstmcell_w_kernel(
                 stop=stop,
             )
 
-        def cols(c):
-            return slice(BANK * c, BANK * (c + 1))
-
-        def pre_act(gate, func, scale, dst):
-            for c in range(NB):
-                pre = pre_pool.tile([P, BANK], F32, name="pre")
-                nc.vector.tensor_tensor(
-                    out=pre[:],
-                    in0=acc[(gate, c)][:],
-                    in1=bias[:, gate * HID + BANK * c : gate * HID + BANK * (c + 1)],
-                    op=ALU.add,
-                )
-                nc.scalar.activation(out=dst[:, cols(c)], in_=pre[:], func=func, scale=scale)
+        def add_bias(gate, c, dst):
+            col = gate * HID + BANK * c
+            nc.vector.tensor_tensor(
+                out=dst, in0=acc[(gate, c)][:], in1=bias[:, col : col + BANK], op=ALU.add
+            )
 
         def after_i_and_f():
-            pre_act(GATE_I, AF.Exp, 1.0, e_s)
-            pre_act(GATE_F, AF.Tanh, 0.5, f_s)
             for c in range(NB):
+                for gate, func, scale, dst in ((GATE_I, AF.Exp, 1.0, e_s), (GATE_F, AF.Tanh, 0.5, f_s)):
+                    pre = pre_pool.tile([P, BANK], F32, name="pre")
+                    add_bias(gate, c, pre[:])
+                    nc.scalar.activation(out=dst[:, cols(c)], in_=pre[:], func=func, scale=scale)
+
+            def f_times(c, new, old):
                 nc.vector.scalar_tensor_tensor(
-                    out=n_new[:, cols(c)], in0=f_s[:, cols(c)], scalar=1.0, in1=n_sb[:, cols(c)],
+                    out=new[:, cols(c)], in0=f_s[:, cols(c)], scalar=1.0, in1=old[:, cols(c)],
                     op0=ALU.add, op1=ALU.mult,
                 )
-                nc.vector.scalar_tensor_tensor(
-                    out=c_new[:, cols(c)], in0=f_s[:, cols(c)], scalar=1.0, in1=c_sb[:, cols(c)],
-                    op0=ALU.add, op1=ALU.mult,
-                )
+
+            def finish_n(c):
                 nc.vector.scalar_tensor_tensor(
                     out=n_new[:, cols(c)], in0=e_s[:, cols(c)], scalar=I_MAX, in1=n_new[:, cols(c)],
                     op0=ALU.min, op1=ALU.add,
@@ -260,83 +267,99 @@ def tile_slstmcell_w_kernel(
                 )
                 nc.scalar.activation(out=rs[:, cols(c)], in_=rs[:, cols(c)], func=AF.Square)
                 nc.scalar.activation(out=rs[:, cols(c)], in_=rs[:, cols(c)], func=AF.Square)
+
+            f_times(0, n_new, n_sb)
+            f_times(1, n_new, n_sb)
+            finish_n(0)
+            f_times(2, n_new, n_sb)
+            finish_n(1)
+            f_times(0, c_new, c_sb)
+            finish_n(2)
+            f_times(1, c_new, c_sb)
+            f_times(2, c_new, c_sb)
+
+        def after_z():
+            for c in range(NB):
+                pre = pre_pool.tile([P, BANK], F32, name="pre")
+                add_bias(GATE_Z, c, pre[:])
+                nc.scalar.activation(out=z_s[:, cols(c)], in_=pre[:], func=AF.Tanh)
             for c in range(NB):
                 nc.vector.scalar_tensor_tensor(
                     out=rs[:, cols(c)], in0=n_new[:, cols(c)], scalar=EPS, in1=rs[:, cols(c)],
                     op0=ALU.add, op1=ALU.mult,
                 )
-
-        def after_z():
-            pre_act(GATE_Z, AF.Tanh, 1.0, z_s)
             for c in range(NB):
                 nc.vector.scalar_tensor_tensor(
                     out=z_s[:, cols(c)], in0=e_s[:, cols(c)], scalar=I_MAX, in1=z_s[:, cols(c)],
                     op0=ALU.min, op1=ALU.mult,
                 )
+            for c in range(NB):
                 nc.vector.tensor_tensor(
                     out=c_new[:, cols(c)], in0=c_new[:, cols(c)], in1=z_s[:, cols(c)], op=ALU.add
                 )
+            for c in range(NB):
                 nc.vector.scalar_tensor_tensor(
                     out=rs[:, cols(c)], in0=rs[:, cols(c)], scalar=0.5, in1=c_new[:, cols(c)],
                     op0=ALU.mult, op1=ALU.mult,
                 )
-            nc.sync.dma_start(out=out_2, in_=n_new[:])
-            nc.sync.dma_start(out=out_1, in_=c_new[:])
 
-        o_s = {}
-        h_new = {}
+        o_s = ep.tile([P, HID], F32, name="o_s")
+        h_new = ep.tile([P, HID], F32, name="h_new")
 
-        def pieces(c):
-            if c == NB - 1:
-                return (slice(0, BANK // 2), slice(BANK // 2, BANK))
-            return (slice(0, BANK),)
+        def halves(c):
+            return (slice(0, BANK // 2), slice(BANK // 2, BANK)) if c == NB - 1 else (slice(0, BANK),)
 
         def o_front(c):
-            pre = tail.tile([P, BANK], F32, name="pre_o")
-            col = GATE_O * HID + BANK * c
-            o_s[c] = tail.tile([P, BANK], F32, name="o_s")
-            for s in pieces(c):
+            for s in halves(c):
+                at = slice(BANK * c + s.start, BANK * c + s.stop)
+                col = GATE_O * HID
                 nc.vector.tensor_tensor(
-                    out=pre[:, s], in0=acc[(GATE_O, c)][:, s], in1=bias[:, col + s.start : col + s.stop], op=ALU.add
+                    out=o_s[:, at], in0=acc[(GATE_O, c)][:, s], in1=bias[:, col + at.start : col + at.stop],
+                    op=ALU.add,
                 )
-                nc.scalar.activation(out=o_s[c][:, s], in_=pre[:, s], func=AF.Tanh, scale=0.5)
+                nc.scalar.activation(out=o_s[:, at], in_=o_s[:, at], func=AF.Tanh, scale=0.5)
 
         def o_back(c):
-            h_new[c] = tail.tile([P, BANK], F32, name="h_new")
-            for s in pieces(c):
+            for s in halves(c):
+                at = slice(BANK * c + s.start, BANK * c + s.stop)
                 nc.vector.scalar_tensor_tensor(
-                    out=h_new[c][:, s], in0=o_s[c][:, s], scalar=1.0,
-                    in1=rs[:, BANK * c + s.start : BANK * c + s.stop], op0=ALU.add, op1=ALU.mult,
+                    out=h_new[:, at], in0=o_s[:, at], scalar=1.0, in1=rs[:, at], op0=ALU.add, op1=ALU.mult
                 )
-            nc.sync.dma_start(out=out_0[:, cols(c)], in_=h_new[c][:])
-
-        after = {"pair": after_i_and_f, GATE_Z: after_z}
 
         for i, step in enumerate(steps):
-            if step[0] == "chunk":
-                c = step[1]
-                wc = loaded[step]
-                for j in range(LAST):
-                    k = NPASS - LAST + j
-                    mx_pass(acc[(GATE_O, c)], k, wc[:, j, :], GATE_O * HID + BANK * c, False, j == LAST - 1)
-                o_front(c)
-                if c > 0:
-                    o_back(c - 1)
+            kind, k = step
+            if kind in ("left", "right"):
+                banks = (0, 1) if kind == "left" else (2,)
+                for c, words in zip(banks, loaded[step]):
+                    mx_pass(acc[(GATE_O, c)], k, words, GATE_O * HID + BANK * c, False, k == NPASS - 1)
             else:
-                k = step[1]
-                wt = loaded[step]
-                gates = (GATE_I, GATE_F) if step[0] == "pair" else (step[0],)
+                gates = (GATE_I, GATE_F) if kind == "pair" else (kind,)
                 for j, gate in enumerate(gates):
                     for c in range(NB):
                         if k == 0:
                             acc[(gate, c)] = psum.tile([P, BANK], F32, name="acc", tag="bank")
                         mx_pass(
-                            acc[(gate, c)], k, wt[:, j * HID + BANK * c : j * HID + BANK * (c + 1)],
+                            acc[(gate, c)], k, loaded[step][:, j * HID + BANK * c : j * HID + BANK * (c + 1)],
                             gate * HID + BANK * c, k == 0, k == NPASS - 1,
                         )
-                if k == NPASS - 1:
-                    after[step[0]]()
             if n_issued <= i + AHEAD and n_issued < len(loads):
                 loads[n_issued]()
                 n_issued += 1
-        o_back(NB - 1)
+            if step == ("pair", NPASS - 1):
+                after_i_and_f()
+            if step == (GATE_Z, NPASS - 1):
+                after_z()
+                while n_issued < len(loads):
+                    loads[n_issued]()
+                    n_issued += 1
+                nc.sync.dma_start(out=out_2, in_=n_new[:])
+                nc.sync.dma_start(out=out_1, in_=c_new[:])
+            if step == ("left", NPASS - 1):
+                o_front(0)
+                o_front(1)
+                o_back(0)
+        o_front(2)
+        o_back(1)
+        nc.sync.dma_start(out=out_0[:, 0 : 2 * BANK], in_=h_new[:, 0 : 2 * BANK])
+        o_back(2)
+        nc.sync.dma_start(out=out_0[:, cols(2)], in_=h_new[:, cols(2)])

@@ -55,8 +55,8 @@ def tile_slstmcell_w_kernel(
         nc.vector.memset(planes_r[:].bitcast(I32), 0)
         b_rows = const.tile([P, BANK], BF16, name="b_rows")
         nc.vector.memset(b_rows[:].bitcast(I32), 0)
-        for q in (0, 2, 1, 3):
-            nc.gpsimd.dma_start(
+        for q in range(4):
+            (nc.scalar if q < 2 else nc.gpsimd).dma_start(
                 out=planes_w[32 * q : 32 * q + 4 * XG, :].bitcast(F32),
                 in_=W_scales[:, 4 * q : 4 * q + 4, :].bitcast(F32),
             )
@@ -71,8 +71,8 @@ def tile_slstmcell_w_kernel(
         )
         ident_b = const.tile([P, P], BF16, name="ident_b")
         nc.vector.tensor_copy(out=ident_b[:], in_=ident_f[:])
-        for q in (0, 2, 1, 3):
-            nc.gpsimd.dma_start(
+        for q in range(4):
+            (nc.scalar if q < 2 else nc.gpsimd).dma_start(
                 out=planes_r[32 * q : 32 * q + 4 * HG, :].bitcast(F32),
                 in_=R_scales[:, 4 * q : 4 * q + 4, :].bitcast(F32),
             )

@@ -25,6 +25,7 @@ APART = 2
 W_BUFS = 9
 AHEAD = 9
 EPS = 1e-6
+DMA_ALIGN = 256
 I_MAX = 50.0
 
 FLOPS = 2 * P * (D_IN + HID) * NCOL
@@ -44,16 +45,16 @@ def tile_slstmcell_w_kernel(
         pre_pool = ctx.enter_context(tc.tile_pool(name="pre_pool", bufs=NB))
         psum = ctx.enter_context(tc.psum_pool(name="psum", bufs=8))
 
-        x_sb = const.tile([P, D_IN], BF16, name="x_sb")
+        x_sb = const.tile([P, D_IN], BF16, name="x_sb", align_bytes=DMA_ALIGN)
         nc.sync.dma_start(out=x_sb[:], in_=x_t)
-        h_sb = const.tile([P, HID], BF16, name="h_sb")
+        h_sb = const.tile([P, HID], BF16, name="h_sb", align_bytes=DMA_ALIGN)
         nc.sync.dma_start(out=h_sb[:], in_=h_prev)
 
-        planes_w = const.tile([P, NCOL], U8, name="planes_w", align_bytes=64)
+        planes_w = const.tile([P, NCOL], U8, name="planes_w", align_bytes=DMA_ALIGN)
         nc.vector.memset(planes_w[:].bitcast(I32), 0)
-        planes_r = const.tile([P, NCOL], U8, name="planes_r", align_bytes=64)
+        planes_r = const.tile([P, NCOL], U8, name="planes_r", align_bytes=DMA_ALIGN)
         nc.vector.memset(planes_r[:].bitcast(I32), 0)
-        b_rows = const.tile([P, BANK], BF16, name="b_rows")
+        b_rows = const.tile([P, BANK], BF16, name="b_rows", align_bytes=DMA_ALIGN)
         nc.vector.memset(b_rows[:].bitcast(I32), 0)
         for q in range(4):
             (nc.scalar if q < 2 else nc.gpsimd).dma_start(
@@ -79,8 +80,8 @@ def tile_slstmcell_w_kernel(
 
         nc.scalar.dma_start(out=b_rows[0 : NCOL // BANK, :], in_=b.rearrange("(m j) -> m j", j=BANK))
 
-        c_sb = const.tile([P, HID], BF16, name="c_sb")
-        n_sb = const.tile([P, HID], BF16, name="n_sb")
+        c_sb = const.tile([P, HID], BF16, name="c_sb", align_bytes=DMA_ALIGN)
+        n_sb = const.tile([P, HID], BF16, name="n_sb", align_bytes=DMA_ALIGN)
 
         def cols(c):
             return slice(BANK * c, BANK * (c + 1))
@@ -96,7 +97,7 @@ def tile_slstmcell_w_kernel(
         def full_load(gate, k):
             def go():
                 src, g = words_of(k)[0:2]
-                wt = wpool.tile([P, HID], I32, name="wt", align_bytes=64)
+                wt = wpool.tile([P, HID], I32, name="wt", align_bytes=DMA_ALIGN)
                 flat = src[g].rearrange("p n t -> p (n t)")
                 nc.sync.dma_start(out=wt[:], in_=flat[:, 4 * gate * HID : 4 * (gate + 1) * HID].bitcast(I32))
                 loaded[(gate, k)] = wt
@@ -106,7 +107,7 @@ def tile_slstmcell_w_kernel(
         def pair_load(k):
             def go():
                 src, g = words_of(k)[0:2]
-                wt = pairpool.tile([P, 2 * HID], I32, name="wp", align_bytes=64)
+                wt = pairpool.tile([P, 2 * HID], I32, name="wp", align_bytes=DMA_ALIGN)
                 flat = src[g].rearrange("p n t -> p (n t)")
                 nc.sync.dma_start(out=wt[:], in_=flat[:, 4 * GATE_I * HID : 4 * (GATE_F + 1) * HID].bitcast(I32))
                 loaded[("pair", k)] = wt
@@ -117,7 +118,7 @@ def tile_slstmcell_w_kernel(
 
         def left_load(k):
             def go():
-                wl = wcpool.tile([P, 2 * BANK], I32, name="wl", align_bytes=64)
+                wl = wcpool.tile([P, 2 * BANK], I32, name="wl", align_bytes=DMA_ALIGN)
                 flat = R_words[k - XG].rearrange("p n t -> p (n t)")
                 col = GATE_O * HID
                 nc.sync.dma_start(out=wl[:], in_=flat[:, 4 * col : 4 * (col + 2 * BANK)].bitcast(I32))
@@ -127,7 +128,7 @@ def tile_slstmcell_w_kernel(
 
         def right_load(k):
             def go():
-                wr = wcpool.tile([P, BANK], I32, name="wr", align_bytes=64)
+                wr = wcpool.tile([P, BANK], I32, name="wr", align_bytes=DMA_ALIGN)
                 flat = R_words[k - XG].rearrange("p n t -> p (n t)")
                 col = GATE_O * HID + 2 * BANK
                 nc.sync.dma_start(out=wr[:], in_=flat[:, 4 * col : 4 * (col + BANK)].bitcast(I32))
@@ -219,12 +220,12 @@ def tile_slstmcell_w_kernel(
         nc.scalar.mul(c_sb[:], c_sb[:], 0.5)
 
         acc = {}
-        f_s = ep.tile([P, HID], F32, name="f_s")
-        e_s = ep.tile([P, HID], F32, name="e_s")
-        z_s = ep.tile([P, HID], F32, name="z_s")
-        n_new = ep.tile([P, HID], F32, name="n_new")
-        c_new = ep.tile([P, HID], F32, name="c_new")
-        rs = ep.tile([P, HID], F32, name="rs")
+        f_s = ep.tile([P, HID], F32, name="f_s", align_bytes=DMA_ALIGN)
+        e_s = ep.tile([P, HID], F32, name="e_s", align_bytes=DMA_ALIGN)
+        z_s = ep.tile([P, HID], F32, name="z_s", align_bytes=DMA_ALIGN)
+        n_new = ep.tile([P, HID], F32, name="n_new", align_bytes=DMA_ALIGN)
+        c_new = ep.tile([P, HID], F32, name="c_new", align_bytes=DMA_ALIGN)
+        rs = ep.tile([P, HID], F32, name="rs", align_bytes=DMA_ALIGN)
 
         def mx_pass(out_bank, k, rhs, col, start, stop):
             g, planes = words_of(k)[1:3]
@@ -303,8 +304,8 @@ def tile_slstmcell_w_kernel(
                     op0=ALU.mult, op1=ALU.mult,
                 )
 
-        o_s = ep.tile([P, HID], F32, name="o_s")
-        h_new = ep.tile([P, HID], F32, name="h_new")
+        o_s = z_s
+        h_new = ep.tile([P, HID], F32, name="h_new", align_bytes=DMA_ALIGN)
 
         def halves(c):
             return (slice(0, BANK // 2), slice(BANK // 2, BANK)) if c == NB - 1 else (slice(0, BANK),)

@@ -22,10 +22,10 @@ HG = HID // 512
 NPASS = XG + HG
 GATE_Z, GATE_I, GATE_F, GATE_O = 0, 1, 2, 3
 APART = 2
-W_BUFS = 9
-AHEAD = 9
+W_BUFS = 8
+AHEAD = 8
 EPS = 1e-6
-DMA_ALIGN = 256
+DMA_ALIGN = 2048
 I_MAX = 50.0
 
 FLOPS = 2 * P * (D_IN + HID) * NCOL
@@ -47,14 +47,14 @@ def tile_slstmcell_w_kernel(
 
         x_sb = const.tile([P, D_IN], BF16, name="x_sb", align_bytes=DMA_ALIGN)
         nc.sync.dma_start(out=x_sb[:], in_=x_t)
-        h_sb = const.tile([P, HID], BF16, name="h_sb", align_bytes=DMA_ALIGN)
+        h_sb = const.tile([P, HID], BF16, name="h_sb", align_bytes=1024)
         nc.sync.dma_start(out=h_sb[:], in_=h_prev)
 
         planes_w = const.tile([P, NCOL], U8, name="planes_w", align_bytes=DMA_ALIGN)
         nc.vector.memset(planes_w[:].bitcast(I32), 0)
         planes_r = const.tile([P, NCOL], U8, name="planes_r", align_bytes=DMA_ALIGN)
         nc.vector.memset(planes_r[:].bitcast(I32), 0)
-        b_rows = const.tile([P, BANK], BF16, name="b_rows", align_bytes=DMA_ALIGN)
+        b_rows = const.tile([P, BANK], BF16, name="b_rows", align_bytes=1024)
         nc.vector.memset(b_rows[:].bitcast(I32), 0)
         for q in range(4):
             (nc.scalar if q < 2 else nc.gpsimd).dma_start(
@@ -80,8 +80,8 @@ def tile_slstmcell_w_kernel(
 
         nc.scalar.dma_start(out=b_rows[0 : NCOL // BANK, :], in_=b.rearrange("(m j) -> m j", j=BANK))
 
-        c_sb = const.tile([P, HID], BF16, name="c_sb", align_bytes=DMA_ALIGN)
-        n_sb = const.tile([P, HID], BF16, name="n_sb", align_bytes=DMA_ALIGN)
+        c_sb = const.tile([P, HID], BF16, name="c_sb", align_bytes=1024)
+        n_sb = const.tile([P, HID], BF16, name="n_sb", align_bytes=1024)
 
         def cols(c):
             return slice(BANK * c, BANK * (c + 1))
@@ -163,10 +163,10 @@ def tile_slstmcell_w_kernel(
                 nc.sync.dma_start(out=n_sb[:], in_=n_prev)
                 nc.sync.dma_start(out=c_sb[:], in_=c_prev)
 
-        grouped = const.tile([P, NPASS * 512], BF16, name="grouped", align_bytes=64)
+        grouped = const.tile([P, NPASS * 512], BF16, name="grouped", align_bytes=256)
         grouped_w = grouped[:].bitcast(F32)
-        codes = const.tile([P, NPASS * P], U32, name="codes", align_bytes=64)
-        xplane = const.tile([P, NPASS * P], U8, name="xplane", align_bytes=64)
+        codes = const.tile([P, NPASS * P], U32, name="codes", align_bytes=256)
+        xplane = const.tile([P, NPASS * P], U8, name="xplane", align_bytes=256)
 
         def transposes(src_sb, g_list):
             bank = psum.tile([P, 4, P], F32, name="tp", tag="bank")
@@ -220,12 +220,12 @@ def tile_slstmcell_w_kernel(
         nc.scalar.mul(c_sb[:], c_sb[:], 0.5)
 
         acc = {}
-        f_s = ep.tile([P, HID], F32, name="f_s", align_bytes=DMA_ALIGN)
-        e_s = ep.tile([P, HID], F32, name="e_s", align_bytes=DMA_ALIGN)
-        z_s = ep.tile([P, HID], F32, name="z_s", align_bytes=DMA_ALIGN)
-        n_new = ep.tile([P, HID], F32, name="n_new", align_bytes=DMA_ALIGN)
-        c_new = ep.tile([P, HID], F32, name="c_new", align_bytes=DMA_ALIGN)
-        rs = ep.tile([P, HID], F32, name="rs", align_bytes=DMA_ALIGN)
+        f_s = ep.tile([P, HID], F32, name="f_s")
+        e_s = ep.tile([P, HID], F32, name="e_s", align_bytes=256)
+        z_s = ep.tile([P, HID], F32, name="z_s", align_bytes=256)
+        n_new = ep.tile([P, HID], F32, name="n_new", align_bytes=256)
+        c_new = ep.tile([P, HID], F32, name="c_new", align_bytes=256)
+        rs = ep.tile([P, HID], F32, name="rs")
 
         def mx_pass(out_bank, k, rhs, col, start, stop):
             g, planes = words_of(k)[1:3]
@@ -305,7 +305,7 @@ def tile_slstmcell_w_kernel(
                 )
 
         o_s = z_s
-        h_new = ep.tile([P, HID], F32, name="h_new", align_bytes=DMA_ALIGN)
+        h_new = e_s
 
         def halves(c):
             return (slice(0, BANK // 2), slice(BANK // 2, BANK)) if c == NB - 1 else (slice(0, BANK),)

@@ -21,11 +21,11 @@ XG = D_IN // 512
 HG = HID // 512
 NPASS = XG + HG
 GATE_Z, GATE_I, GATE_F, GATE_O = 0, 1, 2, 3
-APART = 2
-W_BUFS = 8
-AHEAD = 8
+APART = 1
+W_BUFS = 6
+AHEAD = 6
 EPS = 1e-6
-DMA_ALIGN = 2048
+DMA_ALIGN = 256
 I_MAX = 50.0
 
 FLOPS = 2 * P * (D_IN + HID) * NCOL
@@ -40,21 +40,21 @@ def tile_slstmcell_w_kernel(
         const = ctx.enter_context(tc.tile_pool(name="const", bufs=1))
         wpool = ctx.enter_context(tc.tile_pool(name="wpool", bufs=W_BUFS))
         pairpool = ctx.enter_context(tc.tile_pool(name="pairpool", bufs=NPASS - APART))
-        wcpool = ctx.enter_context(tc.tile_pool(name="wcpool", bufs=NB))
+        wcpool = ctx.enter_context(tc.tile_pool(name="wcpool", bufs=4))
         ep = ctx.enter_context(tc.tile_pool(name="ep", bufs=1))
         pre_pool = ctx.enter_context(tc.tile_pool(name="pre_pool", bufs=NB))
         psum = ctx.enter_context(tc.psum_pool(name="psum", bufs=8))
 
         x_sb = const.tile([P, D_IN], BF16, name="x_sb", align_bytes=DMA_ALIGN)
         nc.sync.dma_start(out=x_sb[:], in_=x_t)
-        h_sb = const.tile([P, HID], BF16, name="h_sb", align_bytes=1024)
+        h_sb = const.tile([P, HID], BF16, name="h_sb", align_bytes=DMA_ALIGN)
         nc.sync.dma_start(out=h_sb[:], in_=h_prev)
 
         planes_w = const.tile([P, NCOL], U8, name="planes_w", align_bytes=DMA_ALIGN)
         nc.vector.memset(planes_w[:].bitcast(I32), 0)
         planes_r = const.tile([P, NCOL], U8, name="planes_r", align_bytes=DMA_ALIGN)
         nc.vector.memset(planes_r[:].bitcast(I32), 0)
-        b_rows = const.tile([P, BANK], BF16, name="b_rows", align_bytes=1024)
+        b_rows = const.tile([P, BANK], BF16, name="b_rows", align_bytes=DMA_ALIGN)
         nc.vector.memset(b_rows[:].bitcast(I32), 0)
         for q in range(4):
             (nc.scalar if q < 2 else nc.gpsimd).dma_start(
@@ -80,8 +80,8 @@ def tile_slstmcell_w_kernel(
 
         nc.scalar.dma_start(out=b_rows[0 : NCOL // BANK, :], in_=b.rearrange("(m j) -> m j", j=BANK))
 
-        c_sb = const.tile([P, HID], BF16, name="c_sb", align_bytes=1024)
-        n_sb = const.tile([P, HID], BF16, name="n_sb", align_bytes=1024)
+        c_sb = const.tile([P, HID], BF16, name="c_sb", align_bytes=DMA_ALIGN)
+        n_sb = const.tile([P, HID], BF16, name="n_sb", align_bytes=DMA_ALIGN)
 
         def cols(c):
             return slice(BANK * c, BANK * (c + 1))
@@ -114,12 +114,13 @@ def tile_slstmcell_w_kernel(
 
             return go
 
-        FULL_O = NPASS - HG
+        FULL_O = NPASS - 4
 
         def left_load(k):
             def go():
+                src, g = words_of(k)[0:2]
                 wl = wcpool.tile([P, 2 * BANK], I32, name="wl", align_bytes=DMA_ALIGN)
-                flat = R_words[k - XG].rearrange("p n t -> p (n t)")
+                flat = src[g].rearrange("p n t -> p (n t)")
                 col = GATE_O * HID
                 nc.sync.dma_start(out=wl[:], in_=flat[:, 4 * col : 4 * (col + 2 * BANK)].bitcast(I32))
                 loaded[("left", k)] = [wl[:, cols(0)], wl[:, cols(1)]]
@@ -128,8 +129,9 @@ def tile_slstmcell_w_kernel(
 
         def right_load(k):
             def go():
+                src, g = words_of(k)[0:2]
                 wr = wcpool.tile([P, BANK], I32, name="wr", align_bytes=DMA_ALIGN)
-                flat = R_words[k - XG].rearrange("p n t -> p (n t)")
+                flat = src[g].rearrange("p n t -> p (n t)")
                 col = GATE_O * HID + 2 * BANK
                 nc.sync.dma_start(out=wr[:], in_=flat[:, 4 * col : 4 * (col + BANK)].bitcast(I32))
                 loaded[("right", k)] = [wr[:]]

@@ -268,8 +268,6 @@ def tile_slstmcell_w_kernel(
                 nc.scalar.activation(
                     out=rs[:, cols(c)], in_=n_new[:, cols(c)], func=AF.Abs_reciprocal_sqrt, bias=eps[:]
                 )
-                nc.scalar.activation(out=rs[:, cols(c)], in_=rs[:, cols(c)], func=AF.Square)
-                nc.scalar.activation(out=rs[:, cols(c)], in_=rs[:, cols(c)], func=AF.Square)
 
             f_times(0, n_new, n_sb)
             f_times(1, n_new, n_sb)
@@ -287,10 +285,8 @@ def tile_slstmcell_w_kernel(
                 add_bias(GATE_Z, c, pre[:])
                 nc.scalar.activation(out=z_s[:, cols(c)], in_=pre[:], func=AF.Tanh)
             for c in range(NB):
-                nc.vector.scalar_tensor_tensor(
-                    out=rs[:, cols(c)], in0=n_new[:, cols(c)], scalar=EPS, in1=rs[:, cols(c)],
-                    op0=ALU.add, op1=ALU.mult,
-                )
+                nc.scalar.activation(out=rs[:, cols(c)], in_=rs[:, cols(c)], func=AF.Square)
+                nc.scalar.activation(out=rs[:, cols(c)], in_=rs[:, cols(c)], func=AF.Square)
             for c in range(NB):
                 nc.vector.scalar_tensor_tensor(
                     out=z_s[:, cols(c)], in0=e_s[:, cols(c)], scalar=I_MAX, in1=z_s[:, cols(c)],
@@ -299,6 +295,11 @@ def tile_slstmcell_w_kernel(
             for c in range(NB):
                 nc.vector.tensor_tensor(
                     out=c_new[:, cols(c)], in0=c_new[:, cols(c)], in1=z_s[:, cols(c)], op=ALU.add
+                )
+            for c in range(NB):
+                nc.vector.scalar_tensor_tensor(
+                    out=rs[:, cols(c)], in0=n_new[:, cols(c)], scalar=EPS, in1=rs[:, cols(c)],
+                    op0=ALU.add, op1=ALU.mult,
                 )
             for c in range(NB):
                 nc.vector.scalar_tensor_tensor(
@@ -361,8 +362,8 @@ def tile_slstmcell_w_kernel(
                 o_front(0)
                 o_front(1)
                 o_back(0)
+                o_back(1)
+                nc.sync.dma_start(out=out_0[:, 0 : 2 * BANK], in_=h_new[:, 0 : 2 * BANK])
         o_front(2)
-        o_back(1)
-        nc.sync.dma_start(out=out_0[:, 0 : 2 * BANK], in_=h_new[:, 0 : 2 * BANK])
         o_back(2)
         nc.sync.dma_start(out=out_0[:, cols(2)], in_=h_new[:, cols(2)])

from contextlib import ExitStack

import concourse.mybir as mybir

F32 = mybir.dt.float32
BF16 = mybir.dt.bfloat16
I32 = mybir.dt.int32
U32 = mybir.dt.uint32
U8 = mybir.dt.uint8
FP8X4 = mybir.dt.float8_e4m3fn_x4
AF = mybir.ActivationFunctionType
ALU = mybir.AluOpType

P = 128
D_IN = 2048
HID = 1536
NCOL = 4 * HID
BANK = 512
NB = HID // BANK
XG = D_IN // 512
HG = HID // 512
NPASS = XG + HG
GATE_Z, GATE_I, GATE_F, GATE_O = 0, 1, 2, 3
APART = 1
W_BUFS = 6
AHEAD = 6
EPS = 1e-6
DMA_ALIGN = 256
I_MAX = 50.0

FLOPS = 2 * P * (D_IN + HID) * NCOL


def tile_slstmcell_w_kernel(
    tc, x_t, h_prev, c_prev, n_prev, W_words, W_scales, R_words, R_scales, b, out_0, out_1, out_2
):
    nc = tc.nc
    with ExitStack() as ctx:
        ctx.enter_context(tc.manual_schedule())
        const = ctx.enter_context(tc.tile_pool(name="const", bufs=1))
        wpool = ctx.enter_context(tc.tile_pool(name="wpool", bufs=W_BUFS))
        pairpool = ctx.enter_context(tc.tile_pool(name="pairpool", bufs=NPASS - APART))
        wcpool = ctx.enter_context(tc.tile_pool(name="wcpool", bufs=4))
        ep = ctx.enter_context(tc.tile_pool(name="ep", bufs=1))
        pre_pool = ctx.enter_context(tc.tile_pool(name="pre_pool", bufs=NB))
        psum = ctx.enter_context(tc.psum_pool(name="psum", bufs=8))

        x_sb = const.tile([P, D_IN], BF16, name="x_sb", align_bytes=DMA_ALIGN)
        nc.sync.dma_start(out=x_sb[:], in_=x_t)
        h_sb = const.tile([P, HID], BF16, name="h_sb", align_bytes=DMA_ALIGN)
        nc.sync.dma_start(out=h_sb[:], in_=h_prev)

        planes_w = const.tile([P, NCOL], U8, name="planes_w", align_bytes=DMA_ALIGN)
        nc.vector.memset(planes_w[:].bitcast(I32), 0)
        planes_r = const.tile([P, NCOL], U8, name="planes_r", align_bytes=DMA_ALIGN)
        nc.vector.memset(planes_r[:].bitcast(I32), 0)
        b_rows = const.tile([P, BANK], BF16, name="b_rows", align_bytes=DMA_ALIGN)
        nc.vector.memset(b_rows[:].bitcast(I32), 0)
        for q in range(4):
            (nc.scalar if q < 2 else nc.gpsimd).dma_start(
                out=planes_w[32 * q : 32 * q + 4 * XG, :].bitcast(F32),
                in_=W_scales[:, 4 * q : 4 * q + 4, :].bitcast(F32),
            )
        eps = const.tile([P, 1], F32, name="eps")
        nc.vector.memset(eps[:], EPS)

        ident_f = const.tile([P, P], F32, name="ident_f")
        nc.vector.memset(ident_f[:], 0.0)
        nc.gpsimd.affine_select(
            out=ident_f[:], in_=ident_f[:], compare_op=ALU.not_equal, fill=1.0, base=0,
            pattern=[[-1, P]], channel_multiplier=1,
        )
        ident_b = const.tile([P, P], BF16, name="ident_b")
        nc.vector.tensor_copy(out=ident_b[:], in_=ident_f[:])
        for q in range(4):
            (nc.scalar if q < 2 else nc.gpsimd).dma_start(
                out=planes_r[32 * q : 32 * q + 4 * HG, :].bitcast(F32),
                in_=R_scales[:, 4 * q : 4 * q + 4, :].bitcast(F32),
            )

        nc.scalar.dma_start(out=b_rows[0 : NCOL // BANK, :], in_=b.rearrange("(m j) -> m j", j=BANK))

        c_sb = const.tile([P, HID], BF16, name="c_sb", align_bytes=DMA_ALIGN)
        n_sb = const.tile([P, HID], BF16, name="n_sb", align_bytes=DMA_ALIGN)

        def cols(c):
            return slice(BANK * c, BANK * (c + 1))

        def words_of(k):
            if k < XG:
                return W_words, k, planes_w
            return R_words, k - XG, planes_r

        loads = []
        loaded = {}

        def full_load(gate, k):
            def go():
                src, g = words_of(k)[0:2]
                wt = wpool.tile([P, HID], I32, name="wt", align_bytes=DMA_ALIGN)
                flat = src[g].rearrange("p n t -> p (n t)")
                nc.sync.dma_start(out=wt[:], in_=flat[:, 4 * gate * HID : 4 * (gate + 1) * HID].bitcast(I32))
                loaded[(gate, k)] = wt

            return go

        def pair_load(k):
            def go():
                src, g = words_of(k)[0:2]
                wt = pairpool.tile([P, 2 * HID], I32, name="wp", align_bytes=DMA_ALIGN)
                flat = src[g].rearrange("p n t -> p (n t)")
                nc.sync.dma_start(out=wt[:], in_=flat[:, 4 * GATE_I * HID : 4 * (GATE_F + 1) * HID].bitcast(I32))
                loaded[("pair", k)] = wt

            return go

        FULL_O = NPASS - 4

        def left_load(k):
            def go():
                src, g = words_of(k)[0:2]
                wl = wcpool.tile([P, 2 * BANK], I32, name="wl", align_bytes=DMA_ALIGN)
                flat = src[g].rearrange("p n t -> p (n t)")
                col = GATE_O * HID
                nc.sync.dma_start(out=wl[:], in_=flat[:, 4 * col : 4 * (col + 2 * BANK)].bitcast(I32))
                loaded[("left", k)] = [wl[:, cols(0)], wl[:, cols(1)]]

            return go

        def right_load(k):
            def go():
                src, g = words_of(k)[0:2]
                wr = wcpool.tile([P, BANK], I32, name="wr", align_bytes=DMA_ALIGN)
                flat = src[g].rearrange("p n t -> p (n t)")
                col = GATE_O * HID + 2 * BANK
                nc.sync.dma_start(out=wr[:], in_=flat[:, 4 * col : 4 * (col + BANK)].bitcast(I32))
                loaded[("right", k)] = [wr[:]]

            return go

        steps = []
        for k in range(APART):
            for gate in (GATE_I, GATE_F):
                loads.append(full_load(gate, k))
                steps.append((gate, k))
        for k in range(APART, NPASS):
            loads.append(pair_load(k))
            steps.append(("pair", k))
        for k in range(NPASS):
            loads.append(full_load(GATE_Z, k))
            steps.append((GATE_Z, k))
        for k in range(FULL_O):
            loads.append(full_load(GATE_O, k))
            steps.append((GATE_O, k))
        for part, load in (("left", left_load), ("right", right_load)):
            for k in range(FULL_O, NPASS):
                loads.append(load(k))
                steps.append((part, k))

        n_issued = 0
        for i in range(NPASS - APART + W_BUFS):
            loads[i]()
            n_issued += 1
            if i == 3:
                nc.sync.dma_start(out=n_sb[:], in_=n_prev)
                nc.sync.dma_start(out=c_sb[:], in_=c_prev)

        grouped = const.tile([P, NPASS * 512], BF16, name="grouped", align_bytes=256)
        grouped_w = grouped[:].bitcast(F32)
        codes = const.tile([P, NPASS * P], U32, name="codes", align_bytes=256)
        xplane = const.tile([P, NPASS * P], U8, name="xplane", align_bytes=256)

        def transposes(src_sb, g_list):
            bank = psum.tile([P, 4, P], F32, name="tp", tag="bank")
            words = src_sb[:].bitcast(F32)
            for j, g in enumerate(g_list):
                for u in range(2):
                    nc.tensor.transpose(bank[:, 2 * j + u, :], words[:, 256 * g + u : 256 * (g + 1) : 2], ident_f[:])
            return bank

        def copy_out(engine_copy, bank, first_pass, n):
            dst = grouped_w[:, 256 * first_pass : 256 * (first_pass + n)].rearrange(
                "p (g r u) -> p g r u", g=n, r=P, u=2
            )
            src = bank[:, 0 : 2 * n, :].rearrange("p (g u) r -> p g r u", g=n, u=2)
            engine_copy(out=dst, in_=src)

        xb0 = transposes(x_sb, [0, 1])
        xb1 = transposes(x_sb, [2, 3])
        hb0 = transposes(h_sb, [0, 1])
        hb1 = transposes(h_sb, [2])
        copy_out(nc.vector.tensor_copy, xb0, 0, 2)
        copy_out(nc.vector.tensor_copy, xb1, 2, 2)
        copy_out(nc.scalar.copy, hb0, 4, 2)
        copy_out(nc.scalar.copy, hb1, 6, 1)

        def quantise(first_pass, n):
            nc.vector.quantize_mx(
                out=codes[:, P * first_pass : P * (first_pass + n)].bitcast(FP8X4),
                scales=xplane[:, P * first_pass : P * (first_pass + n)],
                in_=grouped[:, 512 * first_pass : 512 * (first_pass + n)],
            )

        quantise(0, 4)

        bias = const.tile([P, NCOL], BF16, name="bias")
        for m in range(NCOL // BANK):
            bp = psum.tile([P, BANK], F32, name="bp", tag="bank")
            nc.tensor.matmul(
                out=bp[:], lhsT=ident_b[:, m : m + 1].to_broadcast([P, P]), rhs=b_rows[:], start=True, stop=True
            )
            if m % 2 == 0:
                nc.vector.tensor_copy(out=bias[:, BANK * m : BANK * (m + 1)], in_=bp[:])
            else:
                nc.scalar.copy(out=bias[:, BANK * m : BANK * (m + 1)], in_=bp[:])
            if m == 0:
                quantise(4, 2)
            if m == 2:
                quantise(6, 1)

        nc.scalar.mul(n_sb[:], n_sb[:], 0.5)
        nc.scalar.mul(c_sb[:], c_sb[:], 0.5)

        acc = {}
        f_s = ep.tile([P, HID], F32, name="f_s")
        e_s = ep.tile([P, HID], F32, name="e_s", align_bytes=256)
        z_s = ep.tile([P, HID], F32, name="z_s", align_bytes=256)
        n_new = ep.tile([P, HID], F32, name="n_new", align_bytes=256)
        c_new = ep.tile([P, HID], F32, name="c_new", align_bytes=256)
        rs = ep.tile([P, HID], F32, name="rs")

        def mx_pass(out_bank, k, rhs, col, start, stop):
            g, planes = words_of(k)[1:3]
            nc.tensor.matmul_mx(
                out=out_bank[:],
                lhsT=codes[:, P * k : P * (k + 1)].bitcast(FP8X4),
                lhsT_scale=xplane[:, P * k : P * (k + 1)],
                rhs=rhs.bitcast(FP8X4),
                rhs_scale=planes[4 * g : P, col : col + BANK],
                start=start,
                stop=stop,
            )

        def add_bias(gate, c, dst):
            col = gate * HID + BANK * c
            nc.vector.tensor_tensor(
                out=dst, in0=acc[(gate, c)][:], in1=bias[:, col : col + BANK], op=ALU.add
            )

        def after_i_and_f():
            for c in range(NB):
                for gate, func, scale, dst in ((GATE_I, AF.Exp, 1.0, e_s), (GATE_F, AF.Tanh, 0.5, f_s)):
                    pre = pre_pool.tile([P, BANK], F32, name="pre")
                    add_bias(gate, c, pre[:])
                    nc.scalar.activation(out=dst[:, cols(c)], in_=pre[:], func=func, scale=scale)

            def f_times(c, new, old):
                nc.vector.scalar_tensor_tensor(
                    out=new[:, cols(c)], in0=f_s[:, cols(c)], scalar=1.0, in1=old[:, cols(c)],
                    op0=ALU.add, op1=ALU.mult,
                )

            def finish_n(c):
                nc.vector.scalar_tensor_tensor(
                    out=n_new[:, cols(c)], in0=e_s[:, cols(c)], scalar=I_MAX, in1=n_new[:, cols(c)],
                    op0=ALU.min, op1=ALU.add,
                )
                nc.scalar.activation(
                    out=rs[:, cols(c)], in_=n_new[:, cols(c)], func=AF.Abs_reciprocal_sqrt, bias=eps[:]
                )

            f_times(0, n_new, n_sb)
            f_times(1, n_new, n_sb)
            finish_n(0)
            f_times(2, n_new, n_sb)
            finish_n(1)
            f_times(0, c_new, c_sb)
            finish_n(2)
            f_times(1, c_new, c_sb)
            f_times(2, c_new, c_sb)

        def after_z():
            for c in range(NB):
                pre = pre_pool.tile([P, BANK], F32, name="pre")
                add_bias(GATE_Z, c, pre[:])
                nc.scalar.activation(out=z_s[:, cols(c)], in_=pre[:], func=AF.Tanh)
            for c in range(NB):
                nc.scalar.activation(out=rs[:, cols(c)], in_=rs[:, cols(c)], func=AF.Square)
                nc.scalar.activation(out=rs[:, cols(c)], in_=rs[:, cols(c)], func=AF.Square)
            for c in range(NB):
                nc.vector.scalar_tensor_tensor(
                    out=z_s[:, cols(c)], in0=e_s[:, cols(c)], scalar=I_MAX, in1=z_s[:, cols(c)],
                    op0=ALU.min, op1=ALU.mult,
                )
            for c in range(NB):
                nc.vector.tensor_tensor(
                    out=c_new[:, cols(c)], in0=c_new[:, cols(c)], in1=z_s[:, cols(c)], op=ALU.add
                )
            for c in range(NB):
                nc.vector.scalar_tensor_tensor(
                    out=rs[:, cols(c)], in0=n_new[:, cols(c)], scalar=EPS, in1=rs[:, cols(c)],
                    op0=ALU.add, op1=ALU.mult,
                )
            for c in range(NB):
                nc.vector.scalar_tensor_tensor(
                    out=rs[:, cols(c)], in0=rs[:, cols(c)], scalar=0.5, in1=c_new[:, cols(c)],
                    op0=ALU.mult, op1=ALU.mult,
                )

        o_s = z_s
        h_new = e_s

        def halves(c):
            return (slice(0, BANK // 2), slice(BANK // 2, BANK)) if c == NB - 1 else (slice(0, BANK),)

        def o_front(c):
            for s in halves(c):
                at = slice(BANK * c + s.start, BANK * c + s.stop)
                col = GATE_O * HID
                nc.vector.tensor_tensor(
                    out=o_s[:, at], in0=acc[(GATE_O, c)][:, s], in1=bias[:, col + at.start : col + at.stop],
                    op=ALU.add,
                )
                nc.scalar.activation(out=o_s[:, at], in_=o_s[:, at], func=AF.Tanh, scale=0.5)

        def o_back(c):
            for s in halves(c):
                at = slice(BANK * c + s.start, BANK * c + s.stop)
                nc.vector.scalar_tensor_tensor(
                    out=h_new[:, at], in0=o_s[:, at], scalar=1.0, in1=rs[:, at], op0=ALU.add, op1=ALU.mult
                )

        for i, step in enumerate(steps):
            kind, k = step
            if kind in ("left", "right"):
                banks = (0, 1) if kind == "left" else (2,)
                for c, words in zip(banks, loaded[step]):
                    mx_pass(acc[(GATE_O, c)], k, words, GATE_O * HID + BANK * c, False, k == NPASS - 1)
            else:
                gates = (GATE_I, GATE_F) if kind == "pair" else (kind,)
                for j, gate in enumerate(gates):
                    for c in range(NB):
                        if k == 0:
                            acc[(gate, c)] = psum.tile([P, BANK], F32, name="acc", tag="bank")
                        mx_pass(
                            acc[(gate, c)], k, loaded[step][:, j * HID + BANK * c : j * HID + BANK * (c + 1)],
                            gate * HID + BANK * c, k == 0, k == NPASS - 1,
                        )
            if n_issued <= i + AHEAD and n_issued < len(loads):
                loads[n_issued]()
                n_issued += 1
            if step == ("pair", NPASS - 1):
                after_i_and_f()
            if step == (GATE_Z, NPASS - 1):
                after_z()
                while n_issued < len(loads):
                    loads[n_issued]()
                    n_issued += 1
                nc.sync.dma_start(out=out_2, in_=n_new[:])
                nc.sync.dma_start(out=out_1, in_=c_new[:])
            if step == ("left", NPASS - 1):
                o_front(0)
                o_front(1)
                o_back(0)
                o_back(1)
                nc.sync.dma_start(out=out_0[:, 0 : 2 * BANK], in_=h_new[:, 0 : 2 * BANK])
        o_front(2)
        o_back(2)
        nc.sync.dma_start(out=out_0[:, cols(2)], in_=h_new[:, cols(2)])
